import numpy as np
import ml_dtypes


def mxq(x, axis, fmt="e4m3"):
    dtype, down = {"e4m3": (ml_dtypes.float8_e4m3fn, 7), "e5m2": (ml_dtypes.float8_e5m2, 14)}[fmt]
    v = np.moveaxis(np.asarray(x, np.float32).astype(ml_dtypes.bfloat16).astype(np.float64), axis, -1)
    blocks = v.reshape(v.shape[:-1] + (-1, 32))
    amax = np.abs(blocks).max(-1, keepdims=True)
    byte = np.maximum(np.where(amax > 0, np.frexp(amax)[1] - 1 + 127, 0) - down, 1)
    scale = np.exp2(byte - 127.0)
    codes = (blocks / scale).astype(np.float32).astype(dtype).astype(np.float64)
    return np.moveaxis((codes * scale).reshape(v.shape), -1, axis)


WIDE = False


def mx_kscale(k):
    if not WIDE:
        return np.ones(k)
    levels = np.array([10, -10, 5, -5, 0])
    a = np.random.permutation(np.resize(levels, k // 512 * 4)).reshape(k // 512, 4)
    idx = np.arange(k)
    return np.exp2(a[idx // 512, idx % 128 // 32])


BF16 = ml_dtypes.bfloat16


def bf(x):
    return np.asarray(x, np.float32).astype(BF16)


def f64(x):
    return np.asarray(x).astype(np.float64)


E2M1 = np.array([0.0, 0.5, 1.0, 1.5, 2.0, 3.0, 4.0, 6.0, -0.0, -0.5, -1.0, -1.5, -2.0, -3.0, -4.0, -6.0])


def pack_weight(w, fmt):
    k, n = w.shape
    w = f64(bf(w)).reshape(k // 32, 32, n)
    amax = np.abs(w).max(1)
    if fmt == "e4m3":
        byte = np.frexp(amax)[1] - 1 + 127 - 7
    else:
        mant, ex = np.frexp(amax / 6.0)
        byte = np.where(mant > 0.5, ex, ex - 1) + 127
    byte = np.clip(np.where(amax > 0, byte, 1), 1, 254)
    scaled = (w * np.exp2(127.0 - byte)[:, None, :]).reshape(k, n).astype(np.float32)
    by_word = np.ascontiguousarray(scaled.reshape(k // 512, 128, 4, n).transpose(0, 1, 3, 2))
    if fmt == "e4m3":
        words = by_word.astype(ml_dtypes.float8_e4m3fn).view(np.uint8)
    else:
        c = by_word.astype(ml_dtypes.float4_e2m1fn).view(np.uint8) & 0xF
        words = c[..., 0::2] | (c[..., 1::2] << 4)
    return np.ascontiguousarray(words), np.ascontiguousarray(byte.astype(np.uint8).reshape(k // 512, 16, n))


def unpack_weight(words, scales, fmt):
    g, p, n, _ = words.shape
    if fmt == "e4m3":
        vals = np.ascontiguousarray(words).view(ml_dtypes.float8_e4m3fn).astype(np.float64)
    else:
        nib = np.empty((g, p, n, 4), np.uint8)
        nib[..., 0::2] = words & 0xF
        nib[..., 1::2] = words >> 4
        vals = E2M1[nib]
    vals = vals * np.repeat(np.exp2(scales.astype(np.float64) - 127.0), 8, axis=1)[..., None]
    return vals.transpose(0, 1, 3, 2).reshape(g * 512, n)

def pack4(w):
    words, scales = pack_weight(w, "e2m1")
    return words.reshape(words.shape[0], 128, -1), scales


def unpack4(words, scales):
    return unpack_weight(words.reshape(words.shape[0], 128, -1, 2), scales, "e2m1")


B, SA, SB, D, H, DH = 4, 768, 256, 512, 4, 128
S = SA + SB
EPS = 1e-6


def make_rope(s, dh):
    pos = np.arange(s, dtype=np.float64)
    inv_freq = 1.0 / (10000.0 ** (np.arange(0, dh, 2, dtype=np.float64) / dh))
    theta = pos[:, None] * inv_freq[None, :]
    cos, sin = np.cos(theta), np.sin(theta)
    row0 = np.stack([cos, -sin], axis=-1)
    row1 = np.stack([sin, cos], axis=-1)
    return np.stack([row0, row1], axis=-2)[None, None]


def rms_norm(x, w):
    return x * (1.0 / np.sqrt(np.mean(x * x, axis=-1, keepdims=True) + EPS)) * w


def apply_rope(x, freqs):
    x_ = x.reshape(*x.shape[:-1], -1, 1, 2)
    out = freqs[..., 0] * x_[..., 0] + freqs[..., 1] * x_[..., 1]
    return out.reshape(x.shape)


def qkv(x, w_kn, b):
    y = (mxq(x, 2, "e4m3") @ w_kn) + b
    y = y.reshape(x.shape[0], x.shape[1], 3 * H, DH).transpose(0, 2, 1, 3)
    return y[:, :H], y[:, H:2 * H], y[:, 2 * H:]


def setup_inputs():
    sa, sb = mx_kscale(D), mx_kscale(D)
    hidden_states_a = bf(np.random.standard_normal((B, SA, D)) * sa)
    hidden_states_b = bf(np.random.standard_normal((B, SB, D)) * sb)
    image_rotary_emb = bf(make_rope(S, DH))
    a_w = np.random.standard_normal((3 * D, D)) / np.sqrt(D) / sa
    a_qkv_b = bf(np.random.standard_normal(3 * D) * 0.2)
    b_w = np.random.standard_normal((3 * D, D)) / np.sqrt(D) / sb
    b_qkv_b = bf(np.random.standard_normal(3 * D) * 0.2)
    a_words, a_scales = pack4(np.ascontiguousarray(a_w.T))
    b_words, b_scales = pack4(np.ascontiguousarray(b_w.T))
    return {
        "hidden_states_a": hidden_states_a,
        "hidden_states_b": hidden_states_b,
        "image_rotary_emb": image_rotary_emb,
        "a_qkv_w_words": a_words,
        "a_qkv_w_scales": a_scales,
        "a_qkv_b": a_qkv_b,
        "b_qkv_w_words": b_words,
        "b_qkv_w_scales": b_scales,
        "b_qkv_b": b_qkv_b,
        "norm_q_a_w": bf(1.5 + 0.15 * np.random.standard_normal(DH)),
        "norm_k_a_w": bf(1.5 + 0.15 * np.random.standard_normal(DH)),
        "norm_q_b_w": bf(1.5 + 0.15 * np.random.standard_normal(DH)),
        "norm_k_b_w": bf(1.5 + 0.15 * np.random.standard_normal(DH)),
    }


def reference(hidden_states_a, hidden_states_b, image_rotary_emb, a_qkv_w_words, a_qkv_w_scales, a_qkv_b,
              b_qkv_w_words, b_qkv_w_scales, b_qkv_b, norm_q_a_w, norm_k_a_w, norm_q_b_w, norm_k_b_w):
    q_a, k_a, v_a = qkv(f64(hidden_states_a), unpack4(a_qkv_w_words, a_qkv_w_scales), f64(a_qkv_b))
    q_a = rms_norm(q_a, f64(norm_q_a_w))
    k_a = rms_norm(k_a, f64(norm_k_a_w))
    q_b, k_b, v_b = qkv(f64(hidden_states_b), unpack4(b_qkv_w_words, b_qkv_w_scales), f64(b_qkv_b))
    q_b = rms_norm(q_b, f64(norm_q_b_w))
    k_b = rms_norm(k_b, f64(norm_k_b_w))
    q = np.concatenate([q_b, q_a], axis=2)
    k = np.concatenate([k_b, k_a], axis=2)
    v = np.concatenate([v_b, v_a], axis=2)
    f = f64(image_rotary_emb)
    return apply_rope(q, f), apply_rope(k, f), v

@@ -1,0 +1,490 @@
+from contextlib import ExitStack
+
+import concourse.mybir as mybir
+from concourse.masks import make_identity
+
+F32 = mybir.dt.float32
+BF16 = mybir.dt.bfloat16
+I32 = mybir.dt.int32
+U32 = mybir.dt.uint32
+U8 = mybir.dt.uint8
+FP8X4 = mybir.dt.float8_e4m3fn_x4
+FP4X4 = mybir.dt.float4_e2m1fn_x4
+ACT = mybir.ActivationFunctionType
+ALU = mybir.AluOpType
+
+P = 128
+BATCH = 4
+HEADS = 4
+MODEL_DIM = 512
+OUT_DIM = 3 * MODEL_DIM
+POSITIONS = 1024
+EPS = 1e-6
+PAIRS = P // 2
+CHUNK_TILES = 4
+CHUNK_TOKENS = CHUNK_TILES * P
+QK_SLOTS = 2 * HEADS
+LAG_BIAS = 1
+LAG_TRANSPOSE = 2
+LAG_NORM = 3
+LAG_PRODUCTS = 4
+LAG_SUM = 5
+PREPARE_TICKS = 11
+OUT_GROUP = 4
+KEPT_VALUES = 2
+GAINS_TICK = 1
+
+FLOPS = 2 * BATCH * POSITIONS * MODEL_DIM * OUT_DIM
+
+
+def batch_runs(first_tile, tiles_per_batch):
+    runs = []
+    for k in range(CHUNK_TILES):
+        b, j = divmod(first_tile + k, tiles_per_batch)
+        if runs and runs[-1][2] == b:
+            k0, n = runs[-1][0], runs[-1][1]
+            runs[-1] = (k0, n + 1, b, runs[-1][3])
+        else:
+            runs.append((k, 1, b, j))
+    return runs
+
+
+def tile_fluxjointattention_pa_t_kernel(
+    tc,
+    hidden_states_a,
+    hidden_states_b,
+    image_rotary_emb,
+    a_qkv_w_words,
+    a_qkv_w_scales,
+    a_qkv_b,
+    b_qkv_w_words,
+    b_qkv_w_scales,
+    b_qkv_b,
+    norm_q_a_w,
+    norm_k_a_w,
+    norm_q_b_w,
+    norm_k_b_w,
+    out_0,
+    out_1,
+    out_2,
+):
+    nc = tc.nc
+    stream_a = {
+        "name": "a", "index": 0, "x": hidden_states_a, "words": a_qkv_w_words, "scales": a_qkv_w_scales,
+        "bias": a_qkv_b, "gains": (norm_q_a_w, norm_k_a_w), "tiles_per_batch": 6, "first_position": 256,
+    }
+    stream_b = {
+        "name": "b", "index": 1, "x": hidden_states_b, "words": b_qkv_w_words, "scales": b_qkv_w_scales,
+        "bias": b_qkv_b, "gains": (norm_q_b_w, norm_k_b_w), "tiles_per_batch": 2, "first_position": 0,
+    }
+    streams = (stream_a, stream_b)
+    rope_rows = image_rotary_emb.rearrange("a c s m i l -> (a c s) (m i l)")
+
+    with ExitStack() as pools:
+        const = pools.enter_context(tc.tile_pool(name="const", bufs=1))
+        stage = pools.enter_context(tc.tile_pool(name="stage", bufs=2))
+        codes_pool = pools.enter_context(tc.tile_pool(name="codes", bufs=3))
+        feat_pool = pools.enter_context(tc.tile_pool(name="feat", bufs=3))
+        stat_pool = pools.enter_context(tc.tile_pool(name="stat", bufs=4))
+        prod_pool = pools.enter_context(tc.tile_pool(name="prod", bufs=3))
+        out_pool = pools.enter_context(tc.tile_pool(name="out", bufs=3))
+        values_pool = pools.enter_context(tc.tile_pool(name="values", bufs=2))
+        psum_x = pools.enter_context(tc.psum_pool(name="psum_x", bufs=1))
+        psum_z = pools.enter_context(tc.psum_pool(name="psum_z", bufs=2))
+        psum_y = pools.enter_context(tc.psum_pool(name="psum_y", bufs=4))
+        psum_v = pools.enter_context(tc.psum_pool(name="psum_v", bufs=1))
+
+        for stream in streams:
+            x_sb = const.tile([P, BATCH * stream["tiles_per_batch"], MODEL_DIM], BF16, name="x_" + stream["name"])
+            words_sb = const.tile([P, 2 * OUT_DIM], U8, name="words_" + stream["name"], align_bytes=64)
+            plane_sb = const.tile([P, OUT_DIM], U8, name="plane_" + stream["name"], align_bytes=64)
+            rope_sb = const.tile([P, stream["tiles_per_batch"], 2 * P], BF16, name="rope_" + stream["name"])
+            stream["x_sb"] = x_sb
+            stream["words_sb"] = words_sb
+            stream["plane_sb"] = plane_sb
+            stream["rope_sb"] = rope_sb
+            tables = []
+            for qk in range(2):
+                table = const.tile([P, stream["tiles_per_batch"], 2, P], F32, name="table_" + stream["name"] + "qk"[qk])
+                tables.append(table)
+            stream["tables"] = tables
+        bias_rows = const.tile([P, P], BF16)
+        bias_rows_f32 = const.tile([P, P], F32)
+        bias_columns = const.tile([P, 2 * QK_SLOTS], F32)
+        row_vectors = const.tile([P, 3 * MODEL_DIM], BF16)
+        spread = const.tile([P, 3 * MODEL_DIM], F32)
+        ident = const.tile([P, P], F32)
+        split_pairs = const.tile([P, P], F32)
+        ones = const.tile([P, P], BF16)
+        eps = const.tile([P, 1], F32)
+        first_call = const.tile([P, 1], F32)
+
+        def load_tokens(stream, first_tile, count):
+            j_tiles = stream["tiles_per_batch"]
+            b, j0 = divmod(first_tile, j_tiles)
+            nc.sync.dma_start(
+                out=stream["x_sb"][:, first_tile : first_tile + count, :],
+                in_=stream["x"][b].rearrange("(p j) k -> p j k", j=j_tiles)[:, j0 : j0 + count, :],
+            )
+
+        def load_words(stream):
+            nc.sync.dma_start(out=stream["words_sb"][:].bitcast(I32), in_=stream["words"][0].bitcast(I32))
+
+        def load_scales(stream):
+            for quadrant in range(4):
+                nc.sync.dma_start(
+                    out=stream["plane_sb"][32 * quadrant : 32 * quadrant + 4, :].bitcast(I32),
+                    in_=stream["scales"][0, 4 * quadrant : 4 * quadrant + 4, :].bitcast(I32),
+                )
+
+        def load_rope(stream, queue):
+            first = stream["first_position"]
+            queue.dma_start(
+                out=stream["rope_sb"][:],
+                in_=rope_rows[first : first + P * stream["tiles_per_batch"], :].rearrange(
+                    "(p j) e -> p j e", j=stream["tiles_per_batch"]
+                ),
+            )
+
+        def spread_rows(c, spread_ps):
+            nc.tensor.matmul(
+                out=spread_ps[:], lhsT=ones[:], rhs=row_vectors[:, MODEL_DIM * c : MODEL_DIM * (c + 1)], start=True, stop=True
+            )
+
+        def make_table(stream, qk, l, engine, gains):
+            j_tiles = stream["tiles_per_batch"]
+            column = P * (2 * stream["index"] + qk)
+            gain = gains[:, column : column + P].rearrange("p (m l) -> p l m", l=2)
+            engine.tensor_tensor(
+                out=stream["tables"][qk][:, :, l, :].rearrange("p j (m i) -> p j m i", i=2),
+                in0=stream["rope_sb"][:].rearrange("p j (m i l) -> p j l m i", i=2, l=2)[:, :, l],
+                in1=gain[:, l].unsqueeze(1).unsqueeze(3).to_broadcast([P, j_tiles, PAIRS, 2]),
+                op=ALU.mult,
+            )
+
+        work = [(stream, chunk) for stream in streams for chunk in range(BATCH * stream["tiles_per_batch"] // CHUNK_TILES)]
+        n_heads = QK_SLOTS * len(work)
+        xt_tiles, grouped_tiles, operands, values_ps, values_sb = {}, {}, {}, {}, {}
+        z_tiles, feat_tiles, y_tiles, sum_tiles, inv_tiles, product_tiles, out_tiles, product_groups = {}, {}, {}, {}, {}, {}, {}, {}
+
+        x_bank = psum_x.tile([P, 2, 2, P], F32)
+        head_bank = {}
+
+        def transpose_tokens(w, i):
+            stream, chunk = work[w]
+            if w == 0 and i >= 2:
+                if i == 2:
+                    spare = psum_z.tile([P, 2, 2, P], F32, tag="z")
+                    head_bank[0] = spare
+                xt = head_bank[0][:, i % 2]
+            else:
+                xt = x_bank[:, i % 2]
+            token_words = stream["x_sb"][:, CHUNK_TILES * chunk + i, :].bitcast(F32)
+            for u in range(2):
+                nc.tensor.transpose(out=xt[:, u, :], in_=token_words[:, u : MODEL_DIM // 2 : 2], identity=ident[:])
+            xt_tiles[(w, i)] = xt
+
+        def regroup_tokens(w, i):
+            if i == 0:
+                grouped = stage.tile([P, 4 * CHUNK_TOKENS], BF16, align_bytes=64)
+                grouped_tiles[w] = grouped
+            nc.scalar.copy(
+                out=grouped_tiles[w][:].bitcast(F32)[:, 2 * P * i : 2 * P * (i + 1)].rearrange("p (tok u) -> p tok u", u=2),
+                in_=xt_tiles[(w, i)].rearrange("p u tok -> p tok u"),
+            )
+
+        def quantise_tokens(w, i):
+            if i == 0:
+                codes = codes_pool.tile([P, CHUNK_TOKENS], U32, align_bytes=64)
+                code_scales = codes_pool.tile([P, CHUNK_TOKENS], U8, align_bytes=64)
+                operands[w] = (codes, code_scales)
+            codes, code_scales = operands[w]
+            tokens = slice(P * i, P * (i + 1))
+            nc.vector.quantize_mx(
+                out=codes[:, tokens].bitcast(FP8X4),
+                scales=code_scales[:, tokens],
+                in_=grouped_tiles[w][:, 4 * P * i : 4 * P * (i + 1)],
+            )
+
+        def multiply_values(w, k):
+            if w < 0 or w >= len(work):
+                return
+            stream = work[w][0]
+            codes, code_scales = operands[w]
+            tokens = slice(P * k, P * (k + 1))
+            if w == len(work) - 1 and k == CHUNK_TILES - 1:
+                zv = psum_z.tile([P, MODEL_DIM], F32, tag="z")
+            else:
+                zv = psum_v.tile([P, MODEL_DIM], F32, tag="v")
+            nc.tensor.matmul_mx(
+                out=zv[:],
+                lhsT=codes[:, tokens].bitcast(FP8X4),
+                lhsT_scale=code_scales[:, tokens],
+                rhs=stream["words_sb"][:, 2 * 2 * MODEL_DIM : 2 * OUT_DIM].bitcast(FP4X4),
+                rhs_scale=stream["plane_sb"][:, 2 * MODEL_DIM : OUT_DIM],
+                start=True,
+                stop=True,
+            )
+            values_ps[(w, k)] = zv
+
+        def add_values_bias(w, k):
+            if w < 0 or w >= len(work):
+                return
+            stream, chunk = work[w]
+            s = stream["index"]
+            if k == 0:
+                out_v = values_pool.tile([P, HEADS, CHUNK_TILES, P], F32)
+                values_sb[w] = out_v
+            nc.vector.tensor_tensor(
+                out=values_sb[w][:, :, k, :],
+                in0=values_ps[(w, k)][:].rearrange("p (h f) -> p h f", h=HEADS),
+                in1=spread[:, MODEL_DIM * s : MODEL_DIM * (s + 1)].rearrange("p (h f) -> p h f", h=HEADS),
+                op=ALU.add,
+            )
+            j_tiles = stream["tiles_per_batch"]
+            first = stream["first_position"]
+            for k0, n, b, j0 in batch_runs(CHUNK_TILES * chunk, j_tiles):
+                if k0 + n - 1 == k:
+                    nc.sync.dma_start(
+                        out=out_2[b, :, first : first + P * j_tiles, :].rearrange("h (p j) f -> p h j f", j=j_tiles)[
+                            :, :, j0 : j0 + n, :
+                        ],
+                        in_=values_sb[w][:, :, k0 : k0 + n, :],
+                    )
+
+        def multiply(n):
+            if n < 0 or n >= n_heads:
+                return
+            stream = work[n // QK_SLOTS][0]
+            slot = n % QK_SLOTS
+            codes, code_scales = operands[n // QK_SLOTS]
+            z = psum_z.tile([P, CHUNK_TOKENS], F32, tag="z")
+            nc.tensor.matmul_mx(
+                out=z[:],
+                lhsT=stream["words_sb"][:, 2 * P * slot : 2 * P * (slot + 1)].bitcast(FP4X4),
+                lhsT_scale=stream["plane_sb"][:, P * slot : P * (slot + 1)],
+                rhs=codes[:].bitcast(FP8X4),
+                rhs_scale=code_scales[:],
+                start=True,
+                stop=True,
+            )
+            z_tiles[n] = z
+
+        def add_bias(n):
+            if n < 0 or n >= n_heads:
+                return
+            bias_column = QK_SLOTS * work[n // QK_SLOTS][0]["index"] + n % QK_SLOTS
+            y_feat = feat_pool.tile([P, CHUNK_TOKENS], F32)
+            nc.scalar.activation(
+                out=y_feat[:],
+                in_=z_tiles[n][:],
+                func=ACT.Identity,
+                bias=bias_columns[:, bias_column : bias_column + 1],
+                scale=1.0,
+            )
+            feat_tiles[n] = y_feat
+
+        def transpose_back(n):
+            if n < 0 or n >= n_heads:
+                return
+            y = psum_y.tile([P, CHUNK_TILES, P], F32, tag="y")
+            for k in range(CHUNK_TILES):
+                nc.tensor.transpose(out=y[:, k, :], in_=feat_tiles[n][:, P * k : P * (k + 1)], identity=split_pairs[:])
+            y_tiles[n] = y
+
+        def sum_of_squares(n):
+            if n < 0 or n >= n_heads:
+                return
+            squares = stage.tile([P, CHUNK_TILES, P], F32)
+            sum_squares = stat_pool.tile([P, CHUNK_TILES], F32)
+            for k in range(CHUNK_TILES):
+                nc.scalar.activation(
+                    out=squares[:, k, :], in_=y_tiles[n][:, k, :], func=ACT.Square, accum_out=sum_squares[:, k : k + 1]
+                )
+            sum_tiles[n] = sum_squares
+
+        def inverse_rms(n):
+            if n < 0 or n >= n_heads:
+                return
+            inv_rms = stat_pool.tile([P, CHUNK_TILES], F32)
+            nc.scalar.activation(
+                out=inv_rms[:], in_=sum_tiles[n][:], func=ACT.Abs_reciprocal_sqrt, bias=eps[:, 0:1], scale=1.0 / P
+            )
+            inv_tiles[n] = inv_rms
+
+        def rotation_products(n):
+            if n < 0 or n >= n_heads:
+                return
+            stream, chunk = work[n // QK_SLOTS]
+            table = stream["tables"][(n % QK_SLOTS) // HEADS]
+            if n % OUT_GROUP == 0:
+                products_heads = prod_pool.tile([P, OUT_GROUP, CHUNK_TILES, 2, P], F32)
+                product_groups[n // OUT_GROUP] = products_heads
+            products = product_groups[n // OUT_GROUP][:, n % OUT_GROUP]
+            for k in range(CHUNK_TILES):
+                j = (CHUNK_TILES * chunk + k) % stream["tiles_per_batch"]
+                nc.vector.scalar_tensor_tensor(
+                    out=products[:, k].rearrange("p l (m i) -> p (l m) i", i=2),
+                    in0=y_tiles[n][:, k, :].unsqueeze(2).to_broadcast([P, P, 2]),
+                    scalar=inv_tiles[n][:, k : k + 1],
+                    in1=table[:, j].rearrange("p l (m i) -> p (l m) i", i=2),
+                    op0=ALU.mult,
+                    op1=ALU.mult,
+                )
+            product_tiles[n] = products
+
+        def rotation_sum(n):
+            if n < 0 or n >= n_heads:
+                return
+            stream, chunk = work[n // QK_SLOTS]
+            out_dram = (out_0, out_1)[(n % QK_SLOTS) // HEADS]
+            head = n % HEADS
+            if n % OUT_GROUP == 0:
+                rotated_heads = out_pool.tile([P, OUT_GROUP, CHUNK_TILES, P], F32)
+                out_tiles[n // OUT_GROUP] = rotated_heads
+            rotated = out_tiles[n // OUT_GROUP][:, n % OUT_GROUP]
+            nc.gpsimd.tensor_tensor(
+                out=rotated, in0=product_tiles[n][:, :, 0, :], in1=product_tiles[n][:, :, 1, :], op=ALU.add
+            )
+            j_tiles = stream["tiles_per_batch"]
+            first = stream["first_position"]
+            for k0, count, b, j0 in batch_runs(CHUNK_TILES * chunk, j_tiles):
+                nc.sync.dma_start(
+                    out=out_dram[b, head, first : first + P * j_tiles, :].rearrange("(p j) f -> p j f", j=j_tiles)[
+                        :, j0 : j0 + count, :
+                    ],
+                    in_=rotated[:, k0 : k0 + count, :],
+                )
+
+        def values_ticks(w, k):
+            if w == 0:
+                return k, k
+            if w == len(work) - 1 and k >= CHUNK_TILES - KEPT_VALUES:
+                return n_heads + LAG_PRODUCTS - 1 - (CHUNK_TILES - 1 - k), n_heads + LAG_PRODUCTS
+            return QK_SLOTS * w + 2 * k, QK_SLOTS * w + 2 * k + 1
+
+        multiply_at, add_at = {}, {}
+        for w in range(len(work)):
+            for k in range(CHUNK_TILES):
+                tick_multiply, tick_add = values_ticks(w, k)
+                multiply_at.setdefault(tick_multiply, []).append((w, k))
+                add_at.setdefault(tick_add, []).append((w, k))
+
+        def prepare_ticks(w, i):
+            if w == 1:
+                first = 2 + 2 * (i // 2)
+                return first, first + 1, first + 2
+            first = QK_SLOTS * w - PREPARE_TICKS + 2 * i
+            return first, first + 2, first + 3
+
+        transpose_at, regroup_at, quantise_at = {}, {}, {}
+        last_copy = {}
+        for w in range(1, len(work)):
+            for i in range(CHUNK_TILES):
+                tick_transpose, tick_regroup, tick_quantise = prepare_ticks(w, i)
+                tick_transpose = max(tick_transpose, last_copy.get(i % 2, tick_transpose - 1) + 1)
+                assert tick_transpose < tick_regroup
+                last_copy[i % 2] = tick_regroup
+                transpose_at.setdefault(tick_transpose, []).append((w, i))
+                regroup_at.setdefault(tick_regroup, []).append((w, i))
+                quantise_at.setdefault(tick_quantise, []).append((w, i))
+
+        with tc.manual_schedule():
+            nc.vector.memset(stream_a["plane_sb"][:].bitcast(I32), 0)
+            nc.vector.memset(bias_rows[:], 0.0)
+            nc.vector.memset(row_vectors[:], 0.0)
+            nc.vector.memset(stream_b["plane_sb"][:].bitcast(I32), 0)
+            nc.gpsimd.memset(eps[:], EPS)
+            make_identity(nc, ident[:])
+            nc.gpsimd.memset(ones[:], 1.0)
+
+            nc.scalar.activation(out=first_call[:], in_=eps[:], func=ACT.Abs_reciprocal_sqrt)
+
+            def load_bias_rows(stream):
+                s = stream["index"]
+                nc.sync.dma_start(
+                    out=bias_rows[QK_SLOTS * s : QK_SLOTS * (s + 1), :],
+                    in_=stream["bias"].rearrange("(v f) -> v f", f=P)[0:QK_SLOTS, :],
+                )
+
+            def load_values_bias(stream):
+                s = stream["index"]
+                nc.sync.dma_start(
+                    out=row_vectors[0:1, MODEL_DIM * s : MODEL_DIM * (s + 1)],
+                    in_=stream["bias"][2 * MODEL_DIM : OUT_DIM].unsqueeze(0),
+                )
+
+            load_tokens(stream_a, 0, 2)
+            load_tokens(stream_a, 2, 2)
+            load_scales(stream_a)
+            load_words(stream_a)
+            load_bias_rows(stream_a)
+            load_bias_rows(stream_b)
+            load_values_bias(stream_a)
+            for stream in streams:
+                for qk in range(2):
+                    column = 2 * MODEL_DIM + P * (2 * stream["index"] + qk)
+                    nc.sync.dma_start(out=row_vectors[0:1, column : column + P], in_=stream["gains"][qk].unsqueeze(0))
+            load_rope(stream_a, nc.sync)
+            load_values_bias(stream_b)
+            load_rope(stream_b, nc.sync)
+            load_tokens(stream_a, 4, 2)
+            for b in range(1, BATCH):
+                load_tokens(stream_a, 6 * b, 6)
+            for b in range(BATCH):
+                load_tokens(stream_b, 2 * b, 2)
+            load_words(stream_b)
+            load_scales(stream_b)
+
+            nc.vector.tensor_copy(
+                out=split_pairs[:].rearrange("p (l m) -> p l m", l=2), in_=ident[:].rearrange("p (m l) -> p l m", l=2)
+            )
+            for i in range(CHUNK_TILES):
+                transpose_tokens(0, i)
+            for i in range(CHUNK_TILES):
+                regroup_tokens(0, i)
+            for i in range(CHUNK_TILES):
+                quantise_tokens(0, i)
+            bias_ps = psum_y.tile([P, P], F32, tag="y")
+            values_bias_a_ps = psum_y.tile([P, MODEL_DIM], F32, tag="y")
+            values_bias_b_ps = psum_y.tile([P, MODEL_DIM], F32, tag="y")
+            gains_ps = psum_y.tile([P, MODEL_DIM], F32, tag="y")
+            nc.scalar.copy(out=bias_rows_f32[:], in_=bias_rows[:])
+            nc.tensor.transpose(out=bias_ps[:], in_=bias_rows_f32[:], identity=ident[:])
+            nc.scalar.copy(out=bias_columns[:], in_=bias_ps[:, 0 : 2 * QK_SLOTS])
+            spread_rows(0, values_bias_a_ps)
+            nc.scalar.copy(out=spread[:, 0:MODEL_DIM], in_=values_bias_a_ps[:])
+
+            for tick in range(0, n_heads + LAG_SUM):
+                transpose_back(tick - LAG_TRANSPOSE)
+                for w, i in transpose_at.get(tick, []):
+                    transpose_tokens(w, i)
+                multiply(tick)
+                for w, k in multiply_at.get(tick, []):
+                    multiply_values(w, k)
+                if tick == GAINS_TICK:
+                    spread_rows(2, gains_ps)
+                if tick == GAINS_TICK + 1:
+                    spread_rows(1, values_bias_b_ps)
+                sum_of_squares(tick - LAG_NORM)
+                add_bias(tick - LAG_BIAS)
+                inverse_rms(tick - LAG_NORM)
+                for w, i in regroup_at.get(tick, []):
+                    regroup_tokens(w, i)
+                if tick == GAINS_TICK:
+                    nc.scalar.copy(out=spread[:, 2 * MODEL_DIM : 3 * MODEL_DIM], in_=gains_ps[:])
+                if tick == GAINS_TICK + 1:
+                    nc.scalar.copy(out=spread[:, MODEL_DIM : 2 * MODEL_DIM], in_=values_bias_b_ps[:])
+                rotation_products(tick - LAG_PRODUCTS)
+                for w, k in add_at.get(tick, []):
+                    add_values_bias(w, k)
+                for w, i in quantise_at.get(tick, []):
+                    quantise_tokens(w, i)
+                if 0 <= tick - GAINS_TICK < 3:
+                    stream, qk = ((stream_a, 0), (stream_b, 0), (stream_b, 1))[tick - GAINS_TICK]
+                    for l in range(2):
+                        make_table(stream, qk, l, nc.vector, gains_ps)
+                if tick == GAINS_TICK:
+                    for l in range(2):
+                        make_table(stream_a, 1, l, nc.gpsimd, spread[:, 2 * MODEL_DIM : 3 * MODEL_DIM])
+                rotation_sum(tick - LAG_SUM)

@@ -29,8 +29,9 @@ LAG_TRANSPOSE = 2
 LAG_NORM = 3
 LAG_PRODUCTS = 4
 LAG_SUM = 5
-PREPARE_TICKS = 11
+PREPARE_TICKS = 12
 OUT_GROUP = 4
+SUM_GROUP = 2
 KEPT_VALUES = 2
 GAINS_TICK = 1
 
@@ -333,19 +334,27 @@ def tile_fluxjointattention_pa_t_kernel(
                 )
             product_tiles[n] = products
 
-        def rotation_sum(n):
-            if n < 0 or n >= n_heads:
-                return
+        def rotation_sums(first_head, count):
+            group = first_head // OUT_GROUP
+            if first_head % OUT_GROUP == 0:
+                rotated_heads = out_pool.tile([P, OUT_GROUP, CHUNK_TILES, P], F32)
+                out_tiles[group] = rotated_heads
+            heads = slice(first_head % OUT_GROUP, first_head % OUT_GROUP + count)
+            products = product_groups[group][:, heads].rearrange("p h k l f -> p (h k) l f")
+            nc.gpsimd.tensor_tensor(
+                out=out_tiles[group][:, heads].rearrange("p h k f -> p (h k) f"),
+                in0=products[:, :, 0, :],
+                in1=products[:, :, 1, :],
+                op=ALU.add,
+            )
+            for n in range(first_head, first_head + count):
+                store_head(n)
+
+        def store_head(n):
             stream, chunk = work[n // QK_SLOTS]
             out_dram = (out_0, out_1)[(n % QK_SLOTS) // HEADS]
             head = n % HEADS
-            if n % OUT_GROUP == 0:
-                rotated_heads = out_pool.tile([P, OUT_GROUP, CHUNK_TILES, P], F32)
-                out_tiles[n // OUT_GROUP] = rotated_heads
             rotated = out_tiles[n // OUT_GROUP][:, n % OUT_GROUP]
-            nc.gpsimd.tensor_tensor(
-                out=rotated, in0=product_tiles[n][:, :, 0, :], in1=product_tiles[n][:, :, 1, :], op=ALU.add
-            )
             j_tiles = stream["tiles_per_batch"]
             first = stream["first_position"]
             for k0, count, b, j0 in batch_runs(CHUNK_TILES * chunk, j_tiles):
@@ -361,7 +370,7 @@ def tile_fluxjointattention_pa_t_kernel(
                 return k, k
             if w == len(work) - 1 and k >= CHUNK_TILES - KEPT_VALUES:
                 return n_heads + LAG_PRODUCTS - 1 - (CHUNK_TILES - 1 - k), n_heads + LAG_PRODUCTS
-            return QK_SLOTS * w + 2 * k, QK_SLOTS * w + 2 * k + 1
+            return QK_SLOTS * w + 2 * k + 1, QK_SLOTS * w + 2 * k + 2
 
         multiply_at, add_at = {}, {}
         for w in range(len(work)):
@@ -372,7 +381,7 @@ def tile_fluxjointattention_pa_t_kernel(
 
         def prepare_ticks(w, i):
             if w == 1:
-                first = 2 + 2 * (i // 2)
+                first = 1 + 2 * (i // 2)
                 return first, first + 1, first + 2
             first = QK_SLOTS * w - PREPARE_TICKS + 2 * i
             return first, first + 2, first + 3
@@ -426,10 +435,12 @@ def tile_fluxjointattention_pa_t_kernel(
                     column = 2 * MODEL_DIM + P * (2 * stream["index"] + qk)
                     nc.sync.dma_start(out=row_vectors[0:1, column : column + P], in_=stream["gains"][qk].unsqueeze(0))
             load_rope(stream_a, nc.sync)
+            load_tokens(stream_a, 4, 2)
+            load_tokens(stream_a, 6, 2)
             load_values_bias(stream_b)
             load_rope(stream_b, nc.sync)
-            load_tokens(stream_a, 4, 2)
-            for b in range(1, BATCH):
+            load_tokens(stream_a, 8, 4)
+            for b in range(2, BATCH):
                 load_tokens(stream_a, 6 * b, 6)
             for b in range(BATCH):
                 load_tokens(stream_b, 2 * b, 2)
@@ -487,4 +498,8 @@ def tile_fluxjointattention_pa_t_kernel(
                 if tick == GAINS_TICK:
                     for l in range(2):
                         make_table(stream_a, 1, l, nc.gpsimd, spread[:, 2 * MODEL_DIM : 3 * MODEL_DIM])
-                rotation_sum(tick - LAG_SUM)
+                n = tick - LAG_SUM
+                if n_heads - SUM_GROUP <= n < n_heads:
+                    rotation_sums(n, 1)
+                elif n >= 0 and n % SUM_GROUP == SUM_GROUP - 1:
+                    rotation_sums(n - (SUM_GROUP - 1), SUM_GROUP)

@@ -33,7 +33,7 @@ PREPARE_TICKS = 12
 OUT_GROUP = 4
 SUM_GROUP = 2
 KEPT_VALUES = 2
-GAINS_TICK = 1
+TABLES_TICK = 0
 
 FLOPS = 2 * BATCH * POSITIONS * MODEL_DIM * OUT_DIM
 
@@ -112,8 +112,11 @@ def tile_fluxjointattention_pa_t_kernel(
         bias_rows = const.tile([P, P], BF16)
         bias_rows_f32 = const.tile([P, P], F32)
         bias_columns = const.tile([P, 2 * QK_SLOTS], F32)
-        row_vectors = const.tile([P, 3 * MODEL_DIM], BF16)
-        spread = const.tile([P, 3 * MODEL_DIM], F32)
+        row_vectors = const.tile([P, MODEL_DIM + P], BF16)
+        values_bias_a = const.tile([P, MODEL_DIM], F32)
+        values_bias_b = const.tile([P, MODEL_DIM], BF16)
+        gains_sb = const.tile([P, 4, P], BF16)
+        stream_a["values_bias"], stream_b["values_bias"] = values_bias_a, values_bias_b
         ident = const.tile([P, P], F32)
         split_pairs = const.tile([P, P], F32)
         ones = const.tile([P, P], BF16)
@@ -147,15 +150,12 @@ def tile_fluxjointattention_pa_t_kernel(
                 ),
             )
 
-        def spread_rows(c, spread_ps):
-            nc.tensor.matmul(
-                out=spread_ps[:], lhsT=ones[:], rhs=row_vectors[:, MODEL_DIM * c : MODEL_DIM * (c + 1)], start=True, stop=True
-            )
+        def spread_rows(columns, spread_ps):
+            nc.tensor.matmul(out=spread_ps[:], lhsT=ones[:], rhs=row_vectors[:, columns], start=True, stop=True)
 
-        def make_table(stream, qk, l, engine, gains):
+        def make_table(stream, qk, l, engine, gain_row):
             j_tiles = stream["tiles_per_batch"]
-            column = P * (2 * stream["index"] + qk)
-            gain = gains[:, column : column + P].rearrange("p (m l) -> p l m", l=2)
+            gain = gain_row.rearrange("p (m l) -> p l m", l=2)
             engine.tensor_tensor(
                 out=stream["tables"][qk][:, :, l, :].rearrange("p j (m i) -> p j m i", i=2),
                 in0=stream["rope_sb"][:].rearrange("p j (m i l) -> p j l m i", i=2, l=2)[:, :, l],
@@ -194,17 +194,17 @@ def tile_fluxjointattention_pa_t_kernel(
                 in_=xt_tiles[(w, i)].rearrange("p u tok -> p tok u"),
             )
 
-        def quantise_tokens(w, i):
+        def quantise_tokens(w, i, count):
             if i == 0:
                 codes = codes_pool.tile([P, CHUNK_TOKENS], U32, align_bytes=64)
                 code_scales = codes_pool.tile([P, CHUNK_TOKENS], U8, align_bytes=64)
                 operands[w] = (codes, code_scales)
             codes, code_scales = operands[w]
-            tokens = slice(P * i, P * (i + 1))
+            tokens = slice(P * i, P * (i + count))
             nc.vector.quantize_mx(
                 out=codes[:, tokens].bitcast(FP8X4),
                 scales=code_scales[:, tokens],
-                in_=grouped_tiles[w][:, 4 * P * i : 4 * P * (i + 1)],
+                in_=grouped_tiles[w][:, 4 * P * i : 4 * P * (i + count)],
             )
 
         def multiply_values(w, k):
@@ -232,14 +232,13 @@ def tile_fluxjointattention_pa_t_kernel(
             if w < 0 or w >= len(work):
                 return
             stream, chunk = work[w]
-            s = stream["index"]
             if k == 0:
                 out_v = values_pool.tile([P, HEADS, CHUNK_TILES, P], F32)
                 values_sb[w] = out_v
             nc.vector.tensor_tensor(
                 out=values_sb[w][:, :, k, :],
                 in0=values_ps[(w, k)][:].rearrange("p (h f) -> p h f", h=HEADS),
-                in1=spread[:, MODEL_DIM * s : MODEL_DIM * (s + 1)].rearrange("p (h f) -> p h f", h=HEADS),
+                in1=stream["values_bias"][:].rearrange("p (h f) -> p h f", h=HEADS),
                 op=ALU.add,
             )
             j_tiles = stream["tiles_per_batch"]
@@ -381,22 +380,22 @@ def tile_fluxjointattention_pa_t_kernel(
 
         def prepare_ticks(w, i):
             if w == 1:
-                first = 1 + 2 * (i // 2)
-                return first, first + 1, first + 2
+                first = 2 + 2 * (i // 2)
+                return first, first + 1
             first = QK_SLOTS * w - PREPARE_TICKS + 2 * i
-            return first, first + 2, first + 3
+            return first, first + 2
 
         transpose_at, regroup_at, quantise_at = {}, {}, {}
         last_copy = {}
         for w in range(1, len(work)):
             for i in range(CHUNK_TILES):
-                tick_transpose, tick_regroup, tick_quantise = prepare_ticks(w, i)
+                tick_transpose, tick_regroup = prepare_ticks(w, i)
                 tick_transpose = max(tick_transpose, last_copy.get(i % 2, tick_transpose - 1) + 1)
-                assert tick_transpose < tick_regroup
+                tick_regroup = max(tick_regroup, tick_transpose + 1)
                 last_copy[i % 2] = tick_regroup
                 transpose_at.setdefault(tick_transpose, []).append((w, i))
                 regroup_at.setdefault(tick_regroup, []).append((w, i))
-                quantise_at.setdefault(tick_quantise, []).append((w, i))
+            quantise_at[tick_regroup + 1 - tick_regroup % 2] = w
 
         with tc.manual_schedule():
             nc.vector.memset(stream_a["plane_sb"][:].bitcast(I32), 0)
@@ -411,34 +410,32 @@ def tile_fluxjointattention_pa_t_kernel(
 
             def load_bias_rows(stream):
                 s = stream["index"]
-                nc.sync.dma_start(
+                nc.gpsimd.dma_start(
                     out=bias_rows[QK_SLOTS * s : QK_SLOTS * (s + 1), :],
                     in_=stream["bias"].rearrange("(v f) -> v f", f=P)[0:QK_SLOTS, :],
                 )
 
-            def load_values_bias(stream):
-                s = stream["index"]
+            def spread_gain(stream, qk):
                 nc.sync.dma_start(
-                    out=row_vectors[0:1, MODEL_DIM * s : MODEL_DIM * (s + 1)],
-                    in_=stream["bias"][2 * MODEL_DIM : OUT_DIM].unsqueeze(0),
+                    out=gains_sb[:, 2 * stream["index"] + qk, :], in_=stream["gains"][qk].partition_broadcast(P)
                 )
+
+            load_bias_rows(stream_a)
+            load_bias_rows(stream_b)
+            nc.gpsimd.dma_start(out=row_vectors[0:1, 0:MODEL_DIM], in_=stream_a["bias"][2 * MODEL_DIM : OUT_DIM].unsqueeze(0))
+            nc.gpsimd.dma_start(out=row_vectors[0:1, MODEL_DIM : MODEL_DIM + P], in_=stream_a["gains"][0].unsqueeze(0))
 
             load_tokens(stream_a, 0, 2)
             load_tokens(stream_a, 2, 2)
             load_scales(stream_a)
             load_words(stream_a)
-            load_bias_rows(stream_a)
-            load_bias_rows(stream_b)
-            load_values_bias(stream_a)
-            for stream in streams:
-                for qk in range(2):
-                    column = 2 * MODEL_DIM + P * (2 * stream["index"] + qk)
-                    nc.sync.dma_start(out=row_vectors[0:1, column : column + P], in_=stream["gains"][qk].unsqueeze(0))
             load_rope(stream_a, nc.sync)
             load_tokens(stream_a, 4, 2)
             load_tokens(stream_a, 6, 2)
-            load_values_bias(stream_b)
+            spread_gain(stream_a, 1)
             load_rope(stream_b, nc.sync)
+            spread_gain(stream_b, 0)
+            spread_gain(stream_b, 1)
             load_tokens(stream_a, 8, 4)
             for b in range(2, BATCH):
                 load_tokens(stream_a, 6 * b, 6)
@@ -446,25 +443,28 @@ def tile_fluxjointattention_pa_t_kernel(
                 load_tokens(stream_b, 2 * b, 2)
             load_words(stream_b)
             load_scales(stream_b)
+            nc.sync.dma_start(out=values_bias_b[:], in_=stream_b["bias"][2 * MODEL_DIM : OUT_DIM].partition_broadcast(P))
 
             nc.vector.tensor_copy(
                 out=split_pairs[:].rearrange("p (l m) -> p l m", l=2), in_=ident[:].rearrange("p (m l) -> p l m", l=2)
             )
             for i in range(CHUNK_TILES):
                 transpose_tokens(0, i)
+            bias_ps = psum_y.tile([P, P], F32, tag="y")
+            values_bias_ps = psum_y.tile([P, MODEL_DIM], F32, tag="y")
+            gain_ps = psum_y.tile([P, P], F32, tag="y")
+            spread_rows(slice(0, MODEL_DIM), values_bias_ps)
+            spread_rows(slice(MODEL_DIM, MODEL_DIM + P), gain_ps)
             for i in range(CHUNK_TILES):
                 regroup_tokens(0, i)
-            for i in range(CHUNK_TILES):
-                quantise_tokens(0, i)
-            bias_ps = psum_y.tile([P, P], F32, tag="y")
-            values_bias_a_ps = psum_y.tile([P, MODEL_DIM], F32, tag="y")
-            values_bias_b_ps = psum_y.tile([P, MODEL_DIM], F32, tag="y")
-            gains_ps = psum_y.tile([P, MODEL_DIM], F32, tag="y")
             nc.scalar.copy(out=bias_rows_f32[:], in_=bias_rows[:])
             nc.tensor.transpose(out=bias_ps[:], in_=bias_rows_f32[:], identity=ident[:])
+            nc.scalar.copy(out=values_bias_a[:], in_=values_bias_ps[:])
             nc.scalar.copy(out=bias_columns[:], in_=bias_ps[:, 0 : 2 * QK_SLOTS])
-            spread_rows(0, values_bias_a_ps)
-            nc.scalar.copy(out=spread[:, 0:MODEL_DIM], in_=values_bias_a_ps[:])
+            for i in range(CHUNK_TILES):
+                quantise_tokens(0, i, 1)
+            for l in range(2):
+                make_table(stream_a, 0, l, nc.vector, gain_ps[:])
 
             for tick in range(0, n_heads + LAG_SUM):
                 transpose_back(tick - LAG_TRANSPOSE)
@@ -473,31 +473,20 @@ def tile_fluxjointattention_pa_t_kernel(
                 multiply(tick)
                 for w, k in multiply_at.get(tick, []):
                     multiply_values(w, k)
-                if tick == GAINS_TICK:
-                    spread_rows(2, gains_ps)
-                if tick == GAINS_TICK + 1:
-                    spread_rows(1, values_bias_b_ps)
                 sum_of_squares(tick - LAG_NORM)
                 add_bias(tick - LAG_BIAS)
                 inverse_rms(tick - LAG_NORM)
                 for w, i in regroup_at.get(tick, []):
                     regroup_tokens(w, i)
-                if tick == GAINS_TICK:
-                    nc.scalar.copy(out=spread[:, 2 * MODEL_DIM : 3 * MODEL_DIM], in_=gains_ps[:])
-                if tick == GAINS_TICK + 1:
-                    nc.scalar.copy(out=spread[:, MODEL_DIM : 2 * MODEL_DIM], in_=values_bias_b_ps[:])
                 rotation_products(tick - LAG_PRODUCTS)
                 for w, k in add_at.get(tick, []):
                     add_values_bias(w, k)
-                for w, i in quantise_at.get(tick, []):
-                    quantise_tokens(w, i)
-                if 0 <= tick - GAINS_TICK < 3:
-                    stream, qk = ((stream_a, 0), (stream_b, 0), (stream_b, 1))[tick - GAINS_TICK]
-                    for l in range(2):
-                        make_table(stream, qk, l, nc.vector, gains_ps)
-                if tick == GAINS_TICK:
-                    for l in range(2):
-                        make_table(stream_a, 1, l, nc.gpsimd, spread[:, 2 * MODEL_DIM : 3 * MODEL_DIM])
+                if tick in quantise_at:
+                    quantise_tokens(quantise_at[tick], 0, CHUNK_TILES)
+                if tick == TABLES_TICK:
+                    for stream, qk in ((stream_a, 1), (stream_b, 0), (stream_b, 1)):
+                        for l in range(2):
+                            make_table(stream, qk, l, nc.gpsimd, gains_sb[:, 2 * stream["index"] + qk, :])
                 n = tick - LAG_SUM
                 if n_heads - SUM_GROUP <= n < n_heads:
                     rotation_sums(n, 1)

@@ -34,6 +34,7 @@ OUT_GROUP = 4
 SUM_GROUP = 2
 KEPT_VALUES = 2
 TABLES_TICK = 0
+BIAS_B_TICK = 6
 
 FLOPS = 2 * BATCH * POSITIONS * MODEL_DIM * OUT_DIM
 
@@ -109,13 +110,16 @@ def tile_fluxjointattention_pa_t_kernel(
                 table = const.tile([P, stream["tiles_per_batch"], 2, P], F32, name="table_" + stream["name"] + "qk"[qk])
                 tables.append(table)
             stream["tables"] = tables
-        bias_rows = const.tile([P, P], BF16)
+        for stream in streams:
+            bias_rows = const.tile([P, P], BF16, name="bias_rows_" + stream["name"])
+            stream["bias_rows"] = bias_rows
         bias_rows_f32 = const.tile([P, P], F32)
         bias_columns = const.tile([P, 2 * QK_SLOTS], F32)
-        row_vectors = const.tile([P, MODEL_DIM + P], BF16)
+        row_vectors = const.tile([P, MODEL_DIM + 2 * P], BF16)
         values_bias_a = const.tile([P, MODEL_DIM], F32)
         values_bias_b = const.tile([P, MODEL_DIM], BF16)
-        gains_sb = const.tile([P, 4, P], BF16)
+        key_gain_a = const.tile([P, P], F32)
+        gains_b = const.tile([P, 2, P], BF16)
         stream_a["values_bias"], stream_b["values_bias"] = values_bias_a, values_bias_b
         ident = const.tile([P, P], F32)
         split_pairs = const.tile([P, P], F32)
@@ -215,6 +219,8 @@ def tile_fluxjointattention_pa_t_kernel(
             tokens = slice(P * k, P * (k + 1))
             if w == len(work) - 1 and k == CHUNK_TILES - 1:
                 zv = psum_z.tile([P, MODEL_DIM], F32, tag="z")
+            elif w == 0 and k == 1:
+                zv = values_head_ps
             else:
                 zv = psum_v.tile([P, MODEL_DIM], F32, tag="v")
             nc.tensor.matmul_mx(
@@ -333,14 +339,14 @@ def tile_fluxjointattention_pa_t_kernel(
                 )
             product_tiles[n] = products
 
-        def rotation_sums(first_head, count):
+        def rotation_sums(first_head, count, engine):
             group = first_head // OUT_GROUP
             if first_head % OUT_GROUP == 0:
                 rotated_heads = out_pool.tile([P, OUT_GROUP, CHUNK_TILES, P], F32)
                 out_tiles[group] = rotated_heads
             heads = slice(first_head % OUT_GROUP, first_head % OUT_GROUP + count)
             products = product_groups[group][:, heads].rearrange("p h k l f -> p (h k) l f")
-            nc.gpsimd.tensor_tensor(
+            engine.tensor_tensor(
                 out=out_tiles[group][:, heads].rearrange("p h k f -> p (h k) f"),
                 in0=products[:, :, 0, :],
                 in1=products[:, :, 1, :],
@@ -366,7 +372,7 @@ def tile_fluxjointattention_pa_t_kernel(
 
         def values_ticks(w, k):
             if w == 0:
-                return k, k
+                return ((0, 0), (0, 0), (1, 1), (4, 4))[k]
             if w == len(work) - 1 and k >= CHUNK_TILES - KEPT_VALUES:
                 return n_heads + LAG_PRODUCTS - 1 - (CHUNK_TILES - 1 - k), n_heads + LAG_PRODUCTS
             return QK_SLOTS * w + 2 * k + 1, QK_SLOTS * w + 2 * k + 2
@@ -399,9 +405,10 @@ def tile_fluxjointattention_pa_t_kernel(
 
         with tc.manual_schedule():
             nc.vector.memset(stream_a["plane_sb"][:].bitcast(I32), 0)
-            nc.vector.memset(bias_rows[:], 0.0)
+            nc.vector.memset(stream_a["bias_rows"][:], 0.0)
             nc.vector.memset(row_vectors[:], 0.0)
             nc.vector.memset(stream_b["plane_sb"][:].bitcast(I32), 0)
+            nc.vector.memset(stream_b["bias_rows"][:], 0.0)
             nc.gpsimd.memset(eps[:], EPS)
             make_identity(nc, ident[:])
             nc.gpsimd.memset(ones[:], 1.0)
@@ -409,33 +416,27 @@ def tile_fluxjointattention_pa_t_kernel(
             nc.scalar.activation(out=first_call[:], in_=eps[:], func=ACT.Abs_reciprocal_sqrt)
 
             def load_bias_rows(stream):
-                s = stream["index"]
-                nc.gpsimd.dma_start(
-                    out=bias_rows[QK_SLOTS * s : QK_SLOTS * (s + 1), :],
+                nc.sync.dma_start(
+                    out=stream["bias_rows"][0:QK_SLOTS, :],
                     in_=stream["bias"].rearrange("(v f) -> v f", f=P)[0:QK_SLOTS, :],
                 )
-
-            def spread_gain(stream, qk):
-                nc.sync.dma_start(
-                    out=gains_sb[:, 2 * stream["index"] + qk, :], in_=stream["gains"][qk].partition_broadcast(P)
-                )
-
-            load_bias_rows(stream_a)
-            load_bias_rows(stream_b)
-            nc.gpsimd.dma_start(out=row_vectors[0:1, 0:MODEL_DIM], in_=stream_a["bias"][2 * MODEL_DIM : OUT_DIM].unsqueeze(0))
-            nc.gpsimd.dma_start(out=row_vectors[0:1, MODEL_DIM : MODEL_DIM + P], in_=stream_a["gains"][0].unsqueeze(0))
 
             load_tokens(stream_a, 0, 2)
             load_tokens(stream_a, 2, 2)
             load_scales(stream_a)
             load_words(stream_a)
+            load_bias_rows(stream_a)
+            nc.sync.dma_start(out=row_vectors[0:1, 0:MODEL_DIM], in_=stream_a["bias"][2 * MODEL_DIM : OUT_DIM].unsqueeze(0))
+            for qk in range(2):
+                column = MODEL_DIM + P * qk
+                nc.sync.dma_start(out=row_vectors[0:1, column : column + P], in_=stream_a["gains"][qk].unsqueeze(0))
             load_rope(stream_a, nc.sync)
             load_tokens(stream_a, 4, 2)
             load_tokens(stream_a, 6, 2)
-            spread_gain(stream_a, 1)
             load_rope(stream_b, nc.sync)
-            spread_gain(stream_b, 0)
-            spread_gain(stream_b, 1)
+            for qk in range(2):
+                nc.sync.dma_start(out=gains_b[:, qk, :], in_=stream_b["gains"][qk].partition_broadcast(P))
+            load_bias_rows(stream_b)
             load_tokens(stream_a, 8, 4)
             for b in range(2, BATCH):
                 load_tokens(stream_a, 6 * b, 6)
@@ -452,19 +453,30 @@ def tile_fluxjointattention_pa_t_kernel(
                 transpose_tokens(0, i)
             bias_ps = psum_y.tile([P, P], F32, tag="y")
             values_bias_ps = psum_y.tile([P, MODEL_DIM], F32, tag="y")
-            gain_ps = psum_y.tile([P, P], F32, tag="y")
-            spread_rows(slice(0, MODEL_DIM), values_bias_ps)
-            spread_rows(slice(MODEL_DIM, MODEL_DIM + P), gain_ps)
+            values_head_ps = psum_y.tile([P, MODEL_DIM], F32, tag="y")
+            gains_ps = psum_y.tile([P, 2 * P], F32, tag="y")
             for i in range(CHUNK_TILES):
                 regroup_tokens(0, i)
-            nc.scalar.copy(out=bias_rows_f32[:], in_=bias_rows[:])
-            nc.tensor.transpose(out=bias_ps[:], in_=bias_rows_f32[:], identity=ident[:])
+
+            def copy_bias_rows(stream):
+                nc.scalar.copy(out=bias_rows_f32[:], in_=stream["bias_rows"][:])
+
+            def transpose_bias_rows(bias_columns_ps):
+                nc.tensor.transpose(out=bias_columns_ps[:], in_=bias_rows_f32[:], identity=ident[:])
+
+            def copy_bias_columns(stream, bias_columns_ps):
+                columns = slice(QK_SLOTS * stream["index"], QK_SLOTS * (stream["index"] + 1))
+                nc.scalar.copy(out=bias_columns[:, columns], in_=bias_columns_ps[:, 0:QK_SLOTS])
+
+            copy_bias_rows(stream_a)
+            transpose_bias_rows(bias_ps)
+            copy_bias_columns(stream_a, bias_ps)
+            spread_rows(slice(0, MODEL_DIM), values_bias_ps)
             nc.scalar.copy(out=values_bias_a[:], in_=values_bias_ps[:])
-            nc.scalar.copy(out=bias_columns[:], in_=bias_ps[:, 0 : 2 * QK_SLOTS])
+            spread_rows(slice(MODEL_DIM, MODEL_DIM + 2 * P), gains_ps)
+            nc.scalar.copy(out=key_gain_a[:], in_=gains_ps[:, P : 2 * P])
             for i in range(CHUNK_TILES):
                 quantise_tokens(0, i, 1)
-            for l in range(2):
-                make_table(stream_a, 0, l, nc.vector, gain_ps[:])
 
             for tick in range(0, n_heads + LAG_SUM):
                 transpose_back(tick - LAG_TRANSPOSE)
@@ -473,22 +485,34 @@ def tile_fluxjointattention_pa_t_kernel(
                 multiply(tick)
                 for w, k in multiply_at.get(tick, []):
                     multiply_values(w, k)
+                if tick == BIAS_B_TICK:
+                    bias_b_ps = psum_v.tile([P, P], F32, tag="v")
+                    transpose_bias_rows(bias_b_ps)
                 sum_of_squares(tick - LAG_NORM)
                 add_bias(tick - LAG_BIAS)
                 inverse_rms(tick - LAG_NORM)
+                if tick == BIAS_B_TICK - 1:
+                    copy_bias_rows(stream_b)
+                if tick == BIAS_B_TICK + 1:
+                    copy_bias_columns(stream_b, bias_b_ps)
                 for w, i in regroup_at.get(tick, []):
                     regroup_tokens(w, i)
                 rotation_products(tick - LAG_PRODUCTS)
                 for w, k in add_at.get(tick, []):
                     add_values_bias(w, k)
+                if tick == TABLES_TICK:
+                    for l in range(2):
+                        make_table(stream_a, 0, l, nc.vector, gains_ps[:, 0:P])
+                if tick == n_heads + LAG_PRODUCTS:
+                    rotation_sums(n_heads - 1, 1, nc.vector)
                 if tick in quantise_at:
                     quantise_tokens(quantise_at[tick], 0, CHUNK_TILES)
                 if tick == TABLES_TICK:
-                    for stream, qk in ((stream_a, 1), (stream_b, 0), (stream_b, 1)):
+                    for stream, qk, gain in ((stream_a, 1, key_gain_a[:]), (stream_b, 0, gains_b[:, 0]), (stream_b, 1, gains_b[:, 1])):
                         for l in range(2):
-                            make_table(stream, qk, l, nc.gpsimd, gains_sb[:, 2 * stream["index"] + qk, :])
+                            make_table(stream, qk, l, nc.gpsimd, gain)
                 n = tick - LAG_SUM
-                if n_heads - SUM_GROUP <= n < n_heads:
-                    rotation_sums(n, 1)
-                elif n >= 0 and n % SUM_GROUP == SUM_GROUP - 1:
-                    rotation_sums(n - (SUM_GROUP - 1), SUM_GROUP)
+                if n == n_heads - SUM_GROUP:
+                    rotation_sums(n, 1, nc.gpsimd)
+                elif 0 <= n < n_heads - SUM_GROUP and n % SUM_GROUP == SUM_GROUP - 1:
+                    rotation_sums(n - (SUM_GROUP - 1), SUM_GROUP, nc.gpsimd)

@@ -33,7 +33,7 @@ PREPARE_TICKS = 12
 OUT_GROUP = 4
 SUM_GROUP = 2
 KEPT_VALUES = 2
-TABLES_TICK = 0
+TABLES_TICK = 1
 BIAS_B_TICK = 6
 
 FLOPS = 2 * BATCH * POSITIONS * MODEL_DIM * OUT_DIM
@@ -372,7 +372,7 @@ def tile_fluxjointattention_pa_t_kernel(
 
         def values_ticks(w, k):
             if w == 0:
-                return ((0, 0), (0, 0), (1, 1), (4, 4))[k]
+                return ((0, 0), (0, 0), (2, 2), (4, 4))[k]
             if w == len(work) - 1 and k >= CHUNK_TILES - KEPT_VALUES:
                 return n_heads + LAG_PRODUCTS - 1 - (CHUNK_TILES - 1 - k), n_heads + LAG_PRODUCTS
             return QK_SLOTS * w + 2 * k + 1, QK_SLOTS * w + 2 * k + 2
@@ -402,6 +402,10 @@ def tile_fluxjointattention_pa_t_kernel(
                 transpose_at.setdefault(tick_transpose, []).append((w, i))
                 regroup_at.setdefault(tick_regroup, []).append((w, i))
             quantise_at[tick_regroup + 1 - tick_regroup % 2] = w
+
+        tables_b_at = {}
+        for i in range(4):
+            tables_b_at[QK_SLOTS * (i + 2) - 2] = (i // 2, i % 2)
 
         with tc.manual_schedule():
             nc.vector.memset(stream_a["plane_sb"][:].bitcast(I32), 0)
@@ -473,8 +477,6 @@ def tile_fluxjointattention_pa_t_kernel(
             copy_bias_columns(stream_a, bias_ps)
             spread_rows(slice(0, MODEL_DIM), values_bias_ps)
             nc.scalar.copy(out=values_bias_a[:], in_=values_bias_ps[:])
-            spread_rows(slice(MODEL_DIM, MODEL_DIM + 2 * P), gains_ps)
-            nc.scalar.copy(out=key_gain_a[:], in_=gains_ps[:, P : 2 * P])
             for i in range(CHUNK_TILES):
                 quantise_tokens(0, i, 1)
 
@@ -485,12 +487,16 @@ def tile_fluxjointattention_pa_t_kernel(
                 multiply(tick)
                 for w, k in multiply_at.get(tick, []):
                     multiply_values(w, k)
+                if tick == 0:
+                    spread_rows(slice(MODEL_DIM, MODEL_DIM + 2 * P), gains_ps)
                 if tick == BIAS_B_TICK:
                     bias_b_ps = psum_v.tile([P, P], F32, tag="v")
                     transpose_bias_rows(bias_b_ps)
                 sum_of_squares(tick - LAG_NORM)
                 add_bias(tick - LAG_BIAS)
                 inverse_rms(tick - LAG_NORM)
+                if tick == TABLES_TICK:
+                    nc.scalar.copy(out=key_gain_a[:], in_=gains_ps[:, P : 2 * P])
                 if tick == BIAS_B_TICK - 1:
                     copy_bias_rows(stream_b)
                 if tick == BIAS_B_TICK + 1:
@@ -508,11 +514,13 @@ def tile_fluxjointattention_pa_t_kernel(
                 if tick in quantise_at:
                     quantise_tokens(quantise_at[tick], 0, CHUNK_TILES)
                 if tick == TABLES_TICK:
-                    for stream, qk, gain in ((stream_a, 1, key_gain_a[:]), (stream_b, 0, gains_b[:, 0]), (stream_b, 1, gains_b[:, 1])):
-                        for l in range(2):
-                            make_table(stream, qk, l, nc.gpsimd, gain)
+                    for l in range(2):
+                        make_table(stream_a, 1, l, nc.gpsimd, key_gain_a[:])
                 n = tick - LAG_SUM
                 if n == n_heads - SUM_GROUP:
                     rotation_sums(n, 1, nc.gpsimd)
                 elif 0 <= n < n_heads - SUM_GROUP and n % SUM_GROUP == SUM_GROUP - 1:
                     rotation_sums(n - (SUM_GROUP - 1), SUM_GROUP, nc.gpsimd)
+                if tick in tables_b_at:
+                    qk, l = tables_b_at[tick]
+                    make_table(stream_b, qk, l, nc.gpsimd, gains_b[:, qk])

from contextlib import ExitStack

import concourse.mybir as mybir
from concourse.masks import make_identity

F32 = mybir.dt.float32
BF16 = mybir.dt.bfloat16
I32 = mybir.dt.int32
U32 = mybir.dt.uint32
U8 = mybir.dt.uint8
FP8X4 = mybir.dt.float8_e4m3fn_x4
FP4X4 = mybir.dt.float4_e2m1fn_x4
ACT = mybir.ActivationFunctionType
ALU = mybir.AluOpType

P = 128
BATCH = 4
HEADS = 4
MODEL_DIM = 512
OUT_DIM = 3 * MODEL_DIM
POSITIONS = 1024
EPS = 1e-6
PAIRS = P // 2
CHUNK_TILES = 4
CHUNK_TOKENS = CHUNK_TILES * P
QK_SLOTS = 2 * HEADS
LAG_BIAS = 1
LAG_TRANSPOSE = 2
LAG_NORM = 3
LAG_PRODUCTS = 4
LAG_SUM = 5
PREPARE_TICKS = 12
OUT_GROUP = 4
SUM_GROUP = 2
KEPT_VALUES = 2
TABLES_TICK = 1
BIAS_B_TICK = 6

FLOPS = 2 * BATCH * POSITIONS * MODEL_DIM * OUT_DIM


def batch_runs(first_tile, tiles_per_batch):
    runs = []
    for k in range(CHUNK_TILES):
        b, j = divmod(first_tile + k, tiles_per_batch)
        if runs and runs[-1][2] == b:
            k0, n = runs[-1][0], runs[-1][1]
            runs[-1] = (k0, n + 1, b, runs[-1][3])
        else:
            runs.append((k, 1, b, j))
    return runs


def tile_fluxjointattention_pa_t_kernel(
    tc,
    hidden_states_a,
    hidden_states_b,
    image_rotary_emb,
    a_qkv_w_words,
    a_qkv_w_scales,
    a_qkv_b,
    b_qkv_w_words,
    b_qkv_w_scales,
    b_qkv_b,
    norm_q_a_w,
    norm_k_a_w,
    norm_q_b_w,
    norm_k_b_w,
    out_0,
    out_1,
    out_2,
):
    nc = tc.nc
    stream_a = {
        "name": "a", "index": 0, "x": hidden_states_a, "words": a_qkv_w_words, "scales": a_qkv_w_scales,
        "bias": a_qkv_b, "gains": (norm_q_a_w, norm_k_a_w), "tiles_per_batch": 6, "first_position": 256,
    }
    stream_b = {
        "name": "b", "index": 1, "x": hidden_states_b, "words": b_qkv_w_words, "scales": b_qkv_w_scales,
        "bias": b_qkv_b, "gains": (norm_q_b_w, norm_k_b_w), "tiles_per_batch": 2, "first_position": 0,
    }
    streams = (stream_a, stream_b)
    rope_rows = image_rotary_emb.rearrange("a c s m i l -> (a c s) (m i l)")

    with ExitStack() as pools:
        const = pools.enter_context(tc.tile_pool(name="const", bufs=1))
        stage = pools.enter_context(tc.tile_pool(name="stage", bufs=2))
        codes_pool = pools.enter_context(tc.tile_pool(name="codes", bufs=3))
        feat_pool = pools.enter_context(tc.tile_pool(name="feat", bufs=3))
        stat_pool = pools.enter_context(tc.tile_pool(name="stat", bufs=4))
        prod_pool = pools.enter_context(tc.tile_pool(name="prod", bufs=3))
        out_pool = pools.enter_context(tc.tile_pool(name="out", bufs=3))
        values_pool = pools.enter_context(tc.tile_pool(name="values", bufs=2))
        psum_x = pools.enter_context(tc.psum_pool(name="psum_x", bufs=1))
        psum_z = pools.enter_context(tc.psum_pool(name="psum_z", bufs=2))
        psum_y = pools.enter_context(tc.psum_pool(name="psum_y", bufs=4))
        psum_v = pools.enter_context(tc.psum_pool(name="psum_v", bufs=1))

        for stream in streams:
            x_sb = const.tile([P, BATCH * stream["tiles_per_batch"], MODEL_DIM], BF16, name="x_" + stream["name"])
            words_sb = const.tile([P, 2 * OUT_DIM], U8, name="words_" + stream["name"], align_bytes=64)
            plane_sb = const.tile([P, OUT_DIM], U8, name="plane_" + stream["name"], align_bytes=64)
            rope_sb = const.tile([P, stream["tiles_per_batch"], 2 * P], BF16, name="rope_" + stream["name"])
            stream["x_sb"] = x_sb
            stream["words_sb"] = words_sb
            stream["plane_sb"] = plane_sb
            stream["rope_sb"] = rope_sb
            tables = []
            for qk in range(2):
                table = const.tile([P, stream["tiles_per_batch"], 2, P], F32, name="table_" + stream["name"] + "qk"[qk])
                tables.append(table)
            stream["tables"] = tables
        for stream in streams:
            bias_rows = const.tile([P, P], BF16, name="bias_rows_" + stream["name"])
            stream["bias_rows"] = bias_rows
        bias_rows_f32 = const.tile([P, P], F32)
        bias_columns = const.tile([P, 2 * QK_SLOTS], F32)
        row_vectors = const.tile([P, MODEL_DIM + 2 * P], BF16)
        values_bias_a = const.tile([P, MODEL_DIM], F32)
        values_bias_b = const.tile([P, MODEL_DIM], BF16)
        key_gain_a = const.tile([P, P], F32)
        gains_b = const.tile([P, 2, P], BF16)
        stream_a["values_bias"], stream_b["values_bias"] = values_bias_a, values_bias_b
        ident = const.tile([P, P], F32)
        split_pairs = const.tile([P, P], F32)
        ones = const.tile([P, P], BF16)
        eps = const.tile([P, 1], F32)
        first_call = const.tile([P, 1], F32)

        def load_tokens(stream, first_tile, count):
            j_tiles = stream["tiles_per_batch"]
            b, j0 = divmod(first_tile, j_tiles)
            nc.sync.dma_start(
                out=stream["x_sb"][:, first_tile : first_tile + count, :],
                in_=stream["x"][b].rearrange("(p j) k -> p j k", j=j_tiles)[:, j0 : j0 + count, :],
            )

        def load_words(stream):
            nc.sync.dma_start(out=stream["words_sb"][:].bitcast(I32), in_=stream["words"][0].bitcast(I32))

        def load_scales(stream):
            for quadrant in range(4):
                nc.sync.dma_start(
                    out=stream["plane_sb"][32 * quadrant : 32 * quadrant + 4, :].bitcast(I32),
                    in_=stream["scales"][0, 4 * quadrant : 4 * quadrant + 4, :].bitcast(I32),
                )

        def load_rope(stream, queue):
            first = stream["first_position"]
            queue.dma_start(
                out=stream["rope_sb"][:],
                in_=rope_rows[first : first + P * stream["tiles_per_batch"], :].rearrange(
                    "(p j) e -> p j e", j=stream["tiles_per_batch"]
                ),
            )

        def spread_rows(columns, spread_ps):
            nc.tensor.matmul(out=spread_ps[:], lhsT=ones[:], rhs=row_vectors[:, columns], start=True, stop=True)

        def make_table(stream, qk, l, engine, gain_row):
            j_tiles = stream["tiles_per_batch"]
            gain = gain_row.rearrange("p (m l) -> p l m", l=2)
            engine.tensor_tensor(
                out=stream["tables"][qk][:, :, l, :].rearrange("p j (m i) -> p j m i", i=2),
                in0=stream["rope_sb"][:].rearrange("p j (m i l) -> p j l m i", i=2, l=2)[:, :, l],
                in1=gain[:, l].unsqueeze(1).unsqueeze(3).to_broadcast([P, j_tiles, PAIRS, 2]),
                op=ALU.mult,
            )

        work = [(stream, chunk) for stream in streams for chunk in range(BATCH * stream["tiles_per_batch"] // CHUNK_TILES)]
        n_heads = QK_SLOTS * len(work)
        xt_tiles, grouped_tiles, operands, values_ps, values_sb = {}, {}, {}, {}, {}
        z_tiles, feat_tiles, y_tiles, sum_tiles, inv_tiles, product_tiles, out_tiles, product_groups = {}, {}, {}, {}, {}, {}, {}, {}

        x_bank = psum_x.tile([P, 2, 2, P], F32)
        head_bank = {}

        def transpose_tokens(w, i):
            stream, chunk = work[w]
            if w == 0 and i >= 2:
                if i == 2:
                    spare = psum_z.tile([P, 2, 2, P], F32, tag="z")
                    head_bank[0] = spare
                xt = head_bank[0][:, i % 2]
            else:
                xt = x_bank[:, i % 2]
            token_words = stream["x_sb"][:, CHUNK_TILES * chunk + i, :].bitcast(F32)
            for u in range(2):
                nc.tensor.transpose(out=xt[:, u, :], in_=token_words[:, u : MODEL_DIM // 2 : 2], identity=ident[:])
            xt_tiles[(w, i)] = xt

        def regroup_tokens(w, i):
            if i == 0:
                grouped = stage.tile([P, 4 * CHUNK_TOKENS], BF16, align_bytes=64)
                grouped_tiles[w] = grouped
            nc.scalar.copy(
                out=grouped_tiles[w][:].bitcast(F32)[:, 2 * P * i : 2 * P * (i + 1)].rearrange("p (tok u) -> p tok u", u=2),
                in_=xt_tiles[(w, i)].rearrange("p u tok -> p tok u"),
            )

        def quantise_tokens(w, i, count):
            if i == 0:
                codes = codes_pool.tile([P, CHUNK_TOKENS], U32, align_bytes=64)
                code_scales = codes_pool.tile([P, CHUNK_TOKENS], U8, align_bytes=64)
                operands[w] = (codes, code_scales)
            codes, code_scales = operands[w]
            tokens = slice(P * i, P * (i + count))
            nc.vector.quantize_mx(
                out=codes[:, tokens].bitcast(FP8X4),
                scales=code_scales[:, tokens],
                in_=grouped_tiles[w][:, 4 * P * i : 4 * P * (i + count)],
            )

        def multiply_values(w, k):
            if w < 0 or w >= len(work):
                return
            stream = work[w][0]
            codes, code_scales = operands[w]
            tokens = slice(P * k, P * (k + 1))
            if w == len(work) - 1 and k == CHUNK_TILES - 1:
                zv = psum_z.tile([P, MODEL_DIM], F32, tag="z")
            elif w == 0 and k == 1:
                zv = values_head_ps
            else:
                zv = psum_v.tile([P, MODEL_DIM], F32, tag="v")
            nc.tensor.matmul_mx(
                out=zv[:],
                lhsT=codes[:, tokens].bitcast(FP8X4),
                lhsT_scale=code_scales[:, tokens],
                rhs=stream["words_sb"][:, 2 * 2 * MODEL_DIM : 2 * OUT_DIM].bitcast(FP4X4),
                rhs_scale=stream["plane_sb"][:, 2 * MODEL_DIM : OUT_DIM],
                start=True,
                stop=True,
            )
            values_ps[(w, k)] = zv

        def add_values_bias(w, k):
            if w < 0 or w >= len(work):
                return
            stream, chunk = work[w]
            if k == 0:
                out_v = values_pool.tile([P, HEADS, CHUNK_TILES, P], F32)
                values_sb[w] = out_v
            nc.vector.tensor_tensor(
                out=values_sb[w][:, :, k, :],
                in0=values_ps[(w, k)][:].rearrange("p (h f) -> p h f", h=HEADS),
                in1=stream["values_bias"][:].rearrange("p (h f) -> p h f", h=HEADS),
                op=ALU.add,
            )
            j_tiles = stream["tiles_per_batch"]
            first = stream["first_position"]
            for k0, n, b, j0 in batch_runs(CHUNK_TILES * chunk, j_tiles):
                if k0 + n - 1 == k:
                    nc.sync.dma_start(
                        out=out_2[b, :, first : first + P * j_tiles, :].rearrange("h (p j) f -> p h j f", j=j_tiles)[
                            :, :, j0 : j0 + n, :
                        ],
                        in_=values_sb[w][:, :, k0 : k0 + n, :],
                    )

        def multiply(n):
            if n < 0 or n >= n_heads:
                return
            stream = work[n // QK_SLOTS][0]
            slot = n % QK_SLOTS
            codes, code_scales = operands[n // QK_SLOTS]
            z = psum_z.tile([P, CHUNK_TOKENS], F32, tag="z")
            nc.tensor.matmul_mx(
                out=z[:],
                lhsT=stream["words_sb"][:, 2 * P * slot : 2 * P * (slot + 1)].bitcast(FP4X4),
                lhsT_scale=stream["plane_sb"][:, P * slot : P * (slot + 1)],
                rhs=codes[:].bitcast(FP8X4),
                rhs_scale=code_scales[:],
                start=True,
                stop=True,
            )
            z_tiles[n] = z

        def add_bias(n):
            if n < 0 or n >= n_heads:
                return
            bias_column = QK_SLOTS * work[n // QK_SLOTS][0]["index"] + n % QK_SLOTS
            y_feat = feat_pool.tile([P, CHUNK_TOKENS], F32)
            nc.scalar.activation(
                out=y_feat[:],
                in_=z_tiles[n][:],
                func=ACT.Identity,
                bias=bias_columns[:, bias_column : bias_column + 1],
                scale=1.0,
            )
            feat_tiles[n] = y_feat

        def transpose_back(n):
            if n < 0 or n >= n_heads:
                return
            y = psum_y.tile([P, CHUNK_TILES, P], F32, tag="y")
            for k in range(CHUNK_TILES):
                nc.tensor.transpose(out=y[:, k, :], in_=feat_tiles[n][:, P * k : P * (k + 1)], identity=split_pairs[:])
            y_tiles[n] = y

        def sum_of_squares(n):
            if n < 0 or n >= n_heads:
                return
            squares = stage.tile([P, CHUNK_TILES, P], F32)
            sum_squares = stat_pool.tile([P, CHUNK_TILES], F32)
            for k in range(CHUNK_TILES):
                nc.scalar.activation(
                    out=squares[:, k, :], in_=y_tiles[n][:, k, :], func=ACT.Square, accum_out=sum_squares[:, k : k + 1]
                )
            sum_tiles[n] = sum_squares

        def inverse_rms(n):
            if n < 0 or n >= n_heads:
                return
            inv_rms = stat_pool.tile([P, CHUNK_TILES], F32)
            nc.scalar.activation(
                out=inv_rms[:], in_=sum_tiles[n][:], func=ACT.Abs_reciprocal_sqrt, bias=eps[:, 0:1], scale=1.0 / P
            )
            inv_tiles[n] = inv_rms

        def rotation_products(n):
            if n < 0 or n >= n_heads:
                return
            stream, chunk = work[n // QK_SLOTS]
            table = stream["tables"][(n % QK_SLOTS) // HEADS]
            if n % OUT_GROUP == 0:
                products_heads = prod_pool.tile([P, OUT_GROUP, CHUNK_TILES, 2, P], F32)
                product_groups[n // OUT_GROUP] = products_heads
            products = product_groups[n // OUT_GROUP][:, n % OUT_GROUP]
            for k in range(CHUNK_TILES):
                j = (CHUNK_TILES * chunk + k) % stream["tiles_per_batch"]
                nc.vector.scalar_tensor_tensor(
                    out=products[:, k].rearrange("p l (m i) -> p (l m) i", i=2),
                    in0=y_tiles[n][:, k, :].unsqueeze(2).to_broadcast([P, P, 2]),
                    scalar=inv_tiles[n][:, k : k + 1],
                    in1=table[:, j].rearrange("p l (m i) -> p (l m) i", i=2),
                    op0=ALU.mult,
                    op1=ALU.mult,
                )
            product_tiles[n] = products

        def rotation_sums(first_head, count, engine):
            group = first_head // OUT_GROUP
            if first_head % OUT_GROUP == 0:
                rotated_heads = out_pool.tile([P, OUT_GROUP, CHUNK_TILES, P], F32)
                out_tiles[group] = rotated_heads
            heads = slice(first_head % OUT_GROUP, first_head % OUT_GROUP + count)
            products = product_groups[group][:, heads].rearrange("p h k l f -> p (h k) l f")
            engine.tensor_tensor(
                out=out_tiles[group][:, heads].rearrange("p h k f -> p (h k) f"),
                in0=products[:, :, 0, :],
                in1=products[:, :, 1, :],
                op=ALU.add,
            )
            for n in range(first_head, first_head + count):
                store_head(n)

        def store_head(n):
            stream, chunk = work[n // QK_SLOTS]
            out_dram = (out_0, out_1)[(n % QK_SLOTS) // HEADS]
            head = n % HEADS
            rotated = out_tiles[n // OUT_GROUP][:, n % OUT_GROUP]
            j_tiles = stream["tiles_per_batch"]
            first = stream["first_position"]
            for k0, count, b, j0 in batch_runs(CHUNK_TILES * chunk, j_tiles):
                nc.sync.dma_start(
                    out=out_dram[b, head, first : first + P * j_tiles, :].rearrange("(p j) f -> p j f", j=j_tiles)[
                        :, j0 : j0 + count, :
                    ],
                    in_=rotated[:, k0 : k0 + count, :],
                )

        def values_ticks(w, k):
            if w == 0:
                return ((0, 0), (0, 0), (2, 2), (4, 4))[k]
            if w == len(work) - 1 and k >= CHUNK_TILES - KEPT_VALUES:
                return n_heads + LAG_PRODUCTS - 1 - (CHUNK_TILES - 1 - k), n_heads + LAG_PRODUCTS
            return QK_SLOTS * w + 2 * k + 1, QK_SLOTS * w + 2 * k + 2

        multiply_at, add_at = {}, {}
        for w in range(len(work)):
            for k in range(CHUNK_TILES):
                tick_multiply, tick_add = values_ticks(w, k)
                multiply_at.setdefault(tick_multiply, []).append((w, k))
                add_at.setdefault(tick_add, []).append((w, k))

        def prepare_ticks(w, i):
            if w == 1:
                first = 2 + 2 * (i // 2)
                return first, first + 1
            first = QK_SLOTS * w - PREPARE_TICKS + 2 * i
            return first, first + 2

        transpose_at, regroup_at, quantise_at = {}, {}, {}
        last_copy = {}
        for w in range(1, len(work)):
            for i in range(CHUNK_TILES):
                tick_transpose, tick_regroup = prepare_ticks(w, i)
                tick_transpose = max(tick_transpose, last_copy.get(i % 2, tick_transpose - 1) + 1)
                tick_regroup = max(tick_regroup, tick_transpose + 1)
                last_copy[i % 2] = tick_regroup
                transpose_at.setdefault(tick_transpose, []).append((w, i))
                regroup_at.setdefault(tick_regroup, []).append((w, i))
            quantise_at[tick_regroup + 1 - tick_regroup % 2] = w

        tables_b_at = {}
        for i in range(4):
            tables_b_at[QK_SLOTS * (i + 2) - 2] = (i // 2, i % 2)

        with tc.manual_schedule():
            nc.vector.memset(stream_a["plane_sb"][:].bitcast(I32), 0)
            nc.vector.memset(stream_a["bias_rows"][:], 0.0)
            nc.vector.memset(row_vectors[:], 0.0)
            nc.vector.memset(stream_b["plane_sb"][:].bitcast(I32), 0)
            nc.vector.memset(stream_b["bias_rows"][:], 0.0)
            nc.gpsimd.memset(eps[:], EPS)
            make_identity(nc, ident[:])
            nc.gpsimd.memset(ones[:], 1.0)

            nc.scalar.activation(out=first_call[:], in_=eps[:], func=ACT.Abs_reciprocal_sqrt)

            def load_bias_rows(stream):
                nc.sync.dma_start(
                    out=stream["bias_rows"][0:QK_SLOTS, :],
                    in_=stream["bias"].rearrange("(v f) -> v f", f=P)[0:QK_SLOTS, :],
                )

            load_tokens(stream_a, 0, 2)
            load_tokens(stream_a, 2, 2)
            load_scales(stream_a)
            load_words(stream_a)
            load_bias_rows(stream_a)
            nc.sync.dma_start(out=row_vectors[0:1, 0:MODEL_DIM], in_=stream_a["bias"][2 * MODEL_DIM : OUT_DIM].unsqueeze(0))
            for qk in range(2):
                column = MODEL_DIM + P * qk
                nc.sync.dma_start(out=row_vectors[0:1, column : column + P], in_=stream_a["gains"][qk].unsqueeze(0))
            load_rope(stream_a, nc.sync)
            load_tokens(stream_a, 4, 2)
            load_tokens(stream_a, 6, 2)
            load_rope(stream_b, nc.sync)
            for qk in range(2):
                nc.sync.dma_start(out=gains_b[:, qk, :], in_=stream_b["gains"][qk].partition_broadcast(P))
            load_bias_rows(stream_b)
            load_tokens(stream_a, 8, 4)
            for b in range(2, BATCH):
                load_tokens(stream_a, 6 * b, 6)
            for b in range(BATCH):
                load_tokens(stream_b, 2 * b, 2)
            load_words(stream_b)
            load_scales(stream_b)
            nc.sync.dma_start(out=values_bias_b[:], in_=stream_b["bias"][2 * MODEL_DIM : OUT_DIM].partition_broadcast(P))

            nc.vector.tensor_copy(
                out=split_pairs[:].rearrange("p (l m) -> p l m", l=2), in_=ident[:].rearrange("p (m l) -> p l m", l=2)
            )
            for i in range(CHUNK_TILES):
                transpose_tokens(0, i)
            bias_ps = psum_y.tile([P, P], F32, tag="y")
            values_bias_ps = psum_y.tile([P, MODEL_DIM], F32, tag="y")
            values_head_ps = psum_y.tile([P, MODEL_DIM], F32, tag="y")
            gains_ps = psum_y.tile([P, 2 * P], F32, tag="y")
            for i in range(CHUNK_TILES):
                regroup_tokens(0, i)

            def copy_bias_rows(stream):
                nc.scalar.copy(out=bias_rows_f32[:], in_=stream["bias_rows"][:])

            def transpose_bias_rows(bias_columns_ps):
                nc.tensor.transpose(out=bias_columns_ps[:], in_=bias_rows_f32[:], identity=ident[:])

            def copy_bias_columns(stream, bias_columns_ps):
                columns = slice(QK_SLOTS * stream["index"], QK_SLOTS * (stream["index"] + 1))
                nc.scalar.copy(out=bias_columns[:, columns], in_=bias_columns_ps[:, 0:QK_SLOTS])

            copy_bias_rows(stream_a)
            transpose_bias_rows(bias_ps)
            copy_bias_columns(stream_a, bias_ps)
            spread_rows(slice(0, MODEL_DIM), values_bias_ps)
            nc.scalar.copy(out=values_bias_a[:], in_=values_bias_ps[:])
            for i in range(CHUNK_TILES):
                quantise_tokens(0, i, 1)

            for tick in range(0, n_heads + LAG_SUM):
                transpose_back(tick - LAG_TRANSPOSE)
                for w, i in transpose_at.get(tick, []):
                    transpose_tokens(w, i)
                multiply(tick)
                for w, k in multiply_at.get(tick, []):
                    multiply_values(w, k)
                if tick == 0:
                    spread_rows(slice(MODEL_DIM, MODEL_DIM + 2 * P), gains_ps)
                if tick == BIAS_B_TICK:
                    bias_b_ps = psum_v.tile([P, P], F32, tag="v")
                    transpose_bias_rows(bias_b_ps)
                sum_of_squares(tick - LAG_NORM)
                add_bias(tick - LAG_BIAS)
                inverse_rms(tick - LAG_NORM)
                if tick == TABLES_TICK:
                    nc.scalar.copy(out=key_gain_a[:], in_=gains_ps[:, P : 2 * P])
                if tick == BIAS_B_TICK - 1:
                    copy_bias_rows(stream_b)
                if tick == BIAS_B_TICK + 1:
                    copy_bias_columns(stream_b, bias_b_ps)
                for w, i in regroup_at.get(tick, []):
                    regroup_tokens(w, i)
                rotation_products(tick - LAG_PRODUCTS)
                for w, k in add_at.get(tick, []):
                    add_values_bias(w, k)
                if tick == TABLES_TICK:
                    for l in range(2):
                        make_table(stream_a, 0, l, nc.vector, gains_ps[:, 0:P])
                if tick == n_heads + LAG_PRODUCTS:
                    rotation_sums(n_heads - 1, 1, nc.vector)
                if tick in quantise_at:
                    quantise_tokens(quantise_at[tick], 0, CHUNK_TILES)
                if tick == TABLES_TICK:
                    for l in range(2):
                        make_table(stream_a, 1, l, nc.gpsimd, key_gain_a[:])
                n = tick - LAG_SUM
                if n == n_heads - SUM_GROUP:
                    rotation_sums(n, 1, nc.gpsimd)
                elif 0 <= n < n_heads - SUM_GROUP and n % SUM_GROUP == SUM_GROUP - 1:
                    rotation_sums(n - (SUM_GROUP - 1), SUM_GROUP, nc.gpsimd)
                if tick in tables_b_at:
                    qk, l = tables_b_at[tick]
                    make_table(stream_b, qk, l, nc.gpsimd, gains_b[:, qk])
